import numpy as np
import ml_dtypes


def mxq(x, axis, fmt="e4m3"):
    dtype, down = {"e4m3": (ml_dtypes.float8_e4m3fn, 7), "e5m2": (ml_dtypes.float8_e5m2, 14)}[fmt]
    v = np.moveaxis(np.asarray(x, np.float32).astype(ml_dtypes.bfloat16).astype(np.float64), axis, -1)
    blocks = v.reshape(v.shape[:-1] + (-1, 32))
    amax = np.abs(blocks).max(-1, keepdims=True)
    byte = np.maximum(np.where(amax > 0, np.frexp(amax)[1] - 1 + 127, 0) - down, 1)
    scale = np.exp2(byte - 127.0)
    codes = (blocks / scale).astype(np.float32).astype(dtype).astype(np.float64)
    return np.moveaxis((codes * scale).reshape(v.shape), -1, axis)


BF16 = ml_dtypes.bfloat16


def bf(x):
    return np.asarray(x, np.float32).astype(BF16)


def f64(x):
    return np.asarray(x).astype(np.float64)


N, M, H, D, R = 512, 2048, 8, 512, 4


def draw(rows, u):
    z = np.random.standard_normal((H, rows, R)) * 1.4 / np.sqrt(R)
    g = np.exp(0.5 * np.random.standard_normal((rows, H, 1)))
    v = (z @ u).transpose(1, 0, 2) + np.random.standard_normal((rows, H, D))
    return bf((v * g).reshape(rows, H * D))


def setup_inputs():
    u = np.random.standard_normal((H, R, D))
    return {"batch_s": draw(N, u), "batch_ro": draw(M, u)}


def reference(batch_s, batch_ro):
    s = f64(batch_s).reshape(N, H, D)
    ro = f64(batch_ro).reshape(M, H, D)
    s = s / np.linalg.norm(s, axis=-1, keepdims=True)
    ro = ro / np.linalg.norm(ro, axis=-1, keepdims=True)
    sq = mxq(s, 2, "e4m3")
    roq = mxq(ro, 2, "e4m3")
    dist = sq.transpose(1, 0, 2) @ roq.transpose(1, 2, 0)
    return dist.max(axis=0)

@@ -1,0 +1,181 @@
+from concourse import mybir
+from concourse.masks import make_identity
+
+FLOPS = 2 * 512 * 2048 * 4096
+
+BF16 = mybir.dt.bfloat16
+F32 = mybir.dt.float32
+U32 = mybir.dt.uint32
+U8 = mybir.dt.uint8
+FP8X4 = mybir.dt.float8_e4m3fn_x4
+ACT = mybir.ActivationFunctionType
+ALU = mybir.AluOpType
+
+P = 128
+D = 512
+HEADS = 4
+WIDTH = HEADS * D
+HALVES = 2
+S_TILES = 4
+RO_TILES = 16
+S_ITEMS = S_TILES * HALVES
+ITEMS = (S_TILES + RO_TILES) * HALVES
+AHEAD = 4
+
+
+def tile_multiheaddistance_kernel(tc, batch_s, batch_ro, out):
+    nc = tc.nc
+    out_view = out.rearrange("(n p) m -> p n m", p=P)
+
+    with (
+        tc.tile_pool(name="const", bufs=1) as const,
+        tc.tile_pool(name="raw_pool", bufs=AHEAD + 2) as raw_pool,
+        tc.tile_pool(name="work", bufs=2) as work,
+        tc.tile_pool(name="deep", bufs=3) as deep,
+        tc.tile_pool(name="stats", bufs=4) as stats,
+        tc.psum_pool(name="psum_t", bufs=4) as psum_t,
+        tc.psum_pool(name="psum_mx", bufs=4) as psum_mx,
+        tc.manual_schedule(),
+    ):
+        ident = const.tile([P, P], F32)
+        make_identity(nc, ident[:])
+        one = const.tile([P, 1], F32)
+        nc.vector.memset(one[:], 1.0)
+        warm = const.tile([P, 1], F32)
+        nc.scalar.activation(out=warm[:], in_=one[:], func=ACT.Sqrt)
+
+        s_codes = const.tile([P, S_ITEMS, HEADS * P], U32, align_bytes=64)
+        s_scales = const.tile([P, S_ITEMS, HEADS * P], U8, align_bytes=64)
+
+        raw = {}
+        norm = {}
+        flipped = {}
+        grouped = {}
+        codes = {}
+        scales = {}
+        dist = {}
+        best = {}
+
+        def load(q):
+            tile_index, half = divmod(q, HALVES)
+            cols = slice(half * WIDTH, (half + 1) * WIDTH)
+            if q < S_ITEMS:
+                rows = batch_s[tile_index * P : (tile_index + 1) * P, cols]
+            else:
+                m = tile_index - S_TILES
+                rows = batch_ro[m * P : (m + 1) * P, cols]
+            raw[q] = raw_pool.tile([P, WIDTH], BF16, name="raw")
+            nc.sync.dma_start(out=raw[q][:], in_=rows)
+
+        def norms(q):
+            squares = work.tile([P, WIDTH], BF16, name="squares")
+            sumsq = stats.tile([P, HEADS], F32, name="sumsq")
+            for h in range(HEADS):
+                head = slice(h * D, (h + 1) * D)
+                nc.scalar.activation(
+                    out=squares[:, head], in_=raw[q][:, head], func=ACT.Square,
+                    accum_out=sumsq[:, h : h + 1],
+                )
+            norm[q] = stats.tile([P, HEADS], F32, name="norm")
+            nc.scalar.activation(out=norm[q][:], in_=sumsq[:], func=ACT.Sqrt)
+
+        def scale_and_flip(q):
+            inv_norm = stats.tile([P, HEADS], F32, name="inv_norm")
+            nc.vector.reciprocal(out=inv_norm[:], in_=norm[q][:])
+            unit = work.tile([P, WIDTH], BF16, name="unit")
+            for h in range(HEADS):
+                head = slice(h * D, (h + 1) * D)
+                nc.vector.tensor_scalar(
+                    out=unit[:, head], in0=raw[q][:, head], scalar1=inv_norm[:, h : h + 1],
+                    scalar2=None, op0=ALU.mult,
+                )
+            unit_words = unit[:].bitcast(F32)
+            flipped[q] = []
+            for b in range(HEADS // 2):
+                bank = psum_t.tile([P, 2, 2, P], F32, name="bank")
+                for hh in range(2):
+                    for u in range(2):
+                        first = ((2 * b + hh) * 2 + u) * P
+                        nc.tensor.transpose(
+                            bank[:, hh, u, :], unit_words[:, first : first + P], ident[:]
+                        )
+                flipped[q].append(bank)
+
+        def regroup(q, vector_is_free):
+            grouped[q] = deep.tile([P, WIDTH], BF16, name="grouped", align_bytes=64)
+            words = grouped[q][:].bitcast(F32).rearrange("p (h r u) -> p h r u", h=HEADS, u=2)
+            for b in range(HEADS // 2):
+                dst = words[:, 2 * b : 2 * b + 2, :, :]
+                src = flipped[q][b][:].rearrange("p h u r -> p h r u")
+                if vector_is_free:
+                    nc.vector.tensor_copy(out=dst, in_=src)
+                else:
+                    nc.scalar.copy(out=dst, in_=src)
+
+        def quantise(q):
+            if q < S_ITEMS:
+                codes[q] = s_codes[:, q, :]
+                scales[q] = s_scales[:, q, :]
+            else:
+                ro_codes = deep.tile([P, HEADS * P], U32, name="ro_codes", align_bytes=64)
+                ro_scales = deep.tile([P, HEADS * P], U8, name="ro_scales", align_bytes=64)
+                codes[q] = ro_codes[:]
+                scales[q] = ro_scales[:]
+            nc.vector.quantize_mx(
+                out=codes[q].bitcast(FP8X4), scales=scales[q], in_=grouped[q][:]
+            )
+
+        def products(q):
+            half = q % HALVES
+            dist[q] = []
+            for h in range(HEADS):
+                cols = slice(h * P, (h + 1) * P)
+                bank = psum_mx.tile([P, S_TILES, P], F32, name="dist_bank")
+                for n in range(S_TILES):
+                    nc.tensor.matmul_mx(
+                        out=bank[:, n, :],
+                        lhsT=s_codes[:, n * HALVES + half, cols].bitcast(FP8X4),
+                        lhsT_scale=s_scales[:, n * HALVES + half, cols],
+                        rhs=codes[q][:, cols].bitcast(FP8X4),
+                        rhs_scale=scales[q][:, cols],
+                        start=True,
+                        stop=True,
+                    )
+                dist[q].append(bank)
+
+        def reduce_heads(q):
+            tile_index, half = divmod(q, HALVES)
+            m = tile_index - S_TILES
+            if half == 0:
+                best[m] = deep.tile([P, S_TILES, P], F32, name="best")
+            for h in range(HEADS):
+                for part in range(2):
+                    ns = slice(part * 2, part * 2 + 2)
+                    if half == 0 and h == 0:
+                        nc.vector.tensor_copy(out=best[m][:, ns, :], in_=dist[q][h][:, ns, :])
+                    else:
+                        nc.vector.tensor_tensor(
+                            out=best[m][:, ns, :], in0=dist[q][h][:, ns, :],
+                            in1=best[m][:, ns, :], op=ALU.max,
+                        )
+            if half == HALVES - 1:
+                nc.sync.dma_start(out=out_view[:, :, m * P : (m + 1) * P], in_=best[m][:])
+
+        for q in range(AHEAD):
+            load(q)
+        for slot in range(ITEMS + 3):
+            reducing = S_ITEMS <= slot - 3 < ITEMS
+            if slot + AHEAD < ITEMS:
+                load(slot + AHEAD)
+            if 0 <= slot - 2 < ITEMS:
+                regroup(slot - 2, vector_is_free=not reducing)
+            if slot < ITEMS:
+                norms(slot)
+            if 0 <= slot - 1 < ITEMS:
+                scale_and_flip(slot - 1)
+            if 0 <= slot - 2 < ITEMS:
+                quantise(slot - 2)
+            if reducing:
+                reduce_heads(slot - 3)
+            if S_ITEMS <= slot - 2 < ITEMS:
+                products(slot - 2)

@@ -35,7 +35,6 @@ def tile_multiheaddistance_kernel(tc, batch_s, batch_ro, out):
         tc.tile_pool(name="stats", bufs=4) as stats,
         tc.psum_pool(name="psum_t", bufs=4) as psum_t,
         tc.psum_pool(name="psum_mx", bufs=4) as psum_mx,
-        tc.manual_schedule(),
     ):
         ident = const.tile([P, P], F32)
         make_identity(nc, ident[:])
@@ -48,7 +47,9 @@ def tile_multiheaddistance_kernel(tc, batch_s, batch_ro, out):
         s_scales = const.tile([P, S_ITEMS, HEADS * P], U8, align_bytes=64)
 
         raw = {}
+        sumsq = {}
         norm = {}
+        inv_norm = {}
         flipped = {}
         grouped = {}
         codes = {}
@@ -67,26 +68,30 @@ def tile_multiheaddistance_kernel(tc, batch_s, batch_ro, out):
             raw[q] = raw_pool.tile([P, WIDTH], BF16, name="raw")
             nc.sync.dma_start(out=raw[q][:], in_=rows)
 
-        def norms(q):
+        def sum_squares(q):
             squares = work.tile([P, WIDTH], BF16, name="squares")
-            sumsq = stats.tile([P, HEADS], F32, name="sumsq")
+            sumsq[q] = stats.tile([P, HEADS], F32, name="sumsq")
             for h in range(HEADS):
                 head = slice(h * D, (h + 1) * D)
                 nc.scalar.activation(
                     out=squares[:, head], in_=raw[q][:, head], func=ACT.Square,
-                    accum_out=sumsq[:, h : h + 1],
+                    accum_out=sumsq[q][:, h : h + 1],
                 )
+
+        def root(q):
             norm[q] = stats.tile([P, HEADS], F32, name="norm")
-            nc.scalar.activation(out=norm[q][:], in_=sumsq[:], func=ACT.Sqrt)
+            nc.scalar.activation(out=norm[q][:], in_=sumsq[q][:], func=ACT.Sqrt)
+
+        def invert(q):
+            inv_norm[q] = stats.tile([P, HEADS], F32, name="inv_norm")
+            nc.vector.reciprocal(out=inv_norm[q][:], in_=norm[q][:])
 
         def scale_and_flip(q):
-            inv_norm = stats.tile([P, HEADS], F32, name="inv_norm")
-            nc.vector.reciprocal(out=inv_norm[:], in_=norm[q][:])
             unit = work.tile([P, WIDTH], BF16, name="unit")
             for h in range(HEADS):
                 head = slice(h * D, (h + 1) * D)
                 nc.vector.tensor_scalar(
-                    out=unit[:, head], in0=raw[q][:, head], scalar1=inv_norm[:, h : h + 1],
+                    out=unit[:, head], in0=raw[q][:, head], scalar1=inv_norm[q][:, h : h + 1],
                     scalar2=None, op0=ALU.mult,
                 )
             unit_words = unit[:].bitcast(F32)
@@ -169,12 +174,16 @@ def tile_multiheaddistance_kernel(tc, batch_s, batch_ro, out):
                 load(slot + AHEAD)
             if 0 <= slot - 2 < ITEMS:
                 regroup(slot - 2, vector_is_free=not reducing)
-            if slot < ITEMS:
-                norms(slot)
             if 0 <= slot - 1 < ITEMS:
-                scale_and_flip(slot - 1)
+                root(slot - 1)
+            if slot < ITEMS:
+                sum_squares(slot)
+            if 0 <= slot - 1 < ITEMS:
+                invert(slot - 1)
             if 0 <= slot - 2 < ITEMS:
                 quantise(slot - 2)
+            if 0 <= slot - 1 < ITEMS:
+                scale_and_flip(slot - 1)
             if reducing:
                 reduce_heads(slot - 3)
             if S_ITEMS <= slot - 2 < ITEMS:

@@ -154,14 +154,13 @@ def tile_multiheaddistance_kernel(tc, batch_s, batch_ro, out):
             if half == 0:
                 best[m] = deep.tile([P, S_TILES, P], F32, name="best")
             for h in range(HEADS):
-                for part in range(2):
-                    ns = slice(part * 2, part * 2 + 2)
+                for n in range(S_TILES):
                     if half == 0 and h == 0:
-                        nc.vector.tensor_copy(out=best[m][:, ns, :], in_=dist[q][h][:, ns, :])
+                        nc.vector.tensor_copy(out=best[m][:, n, :], in_=dist[q][h][:, n, :])
                     else:
                         nc.vector.tensor_tensor(
-                            out=best[m][:, ns, :], in0=dist[q][h][:, ns, :],
-                            in1=best[m][:, ns, :], op=ALU.max,
+                            out=best[m][:, n, :], in0=dist[q][h][:, n, :],
+                            in1=best[m][:, n, :], op=ALU.max,
                         )
             if half == HALVES - 1:
                 nc.sync.dma_start(out=out_view[:, :, m * P : (m + 1) * P], in_=best[m][:])

@@ -41,14 +41,13 @@ def tile_multiheaddistance_kernel(tc, batch_s, batch_ro, out):
         one = const.tile([P, 1], F32)
         nc.vector.memset(one[:], 1.0)
         warm = const.tile([P, 1], F32)
-        nc.scalar.activation(out=warm[:], in_=one[:], func=ACT.Sqrt)
+        nc.scalar.activation(out=warm[:], in_=one[:], func=ACT.Abs_reciprocal_sqrt)
 
         s_codes = const.tile([P, S_ITEMS, HEADS * P], U32, align_bytes=64)
         s_scales = const.tile([P, S_ITEMS, HEADS * P], U8, align_bytes=64)
 
         raw = {}
         sumsq = {}
-        norm = {}
         inv_norm = {}
         flipped = {}
         grouped = {}
@@ -78,13 +77,11 @@ def tile_multiheaddistance_kernel(tc, batch_s, batch_ro, out):
                     accum_out=sumsq[q][:, h : h + 1],
                 )
 
-        def root(q):
-            norm[q] = stats.tile([P, HEADS], F32, name="norm")
-            nc.scalar.activation(out=norm[q][:], in_=sumsq[q][:], func=ACT.Sqrt)
-
-        def invert(q):
+        def invert_root(q):
             inv_norm[q] = stats.tile([P, HEADS], F32, name="inv_norm")
-            nc.vector.reciprocal(out=inv_norm[q][:], in_=norm[q][:])
+            nc.scalar.activation(
+                out=inv_norm[q][:], in_=sumsq[q][:], func=ACT.Abs_reciprocal_sqrt
+            )
 
         def scale_and_flip(q):
             unit = work.tile([P, WIDTH], BF16, name="unit")
@@ -174,11 +171,9 @@ def tile_multiheaddistance_kernel(tc, batch_s, batch_ro, out):
             if 0 <= slot - 2 < ITEMS:
                 regroup(slot - 2, vector_is_free=not reducing)
             if 0 <= slot - 1 < ITEMS:
-                root(slot - 1)
+                invert_root(slot - 1)
             if slot < ITEMS:
                 sum_squares(slot)
-            if 0 <= slot - 1 < ITEMS:
-                invert(slot - 1)
             if 0 <= slot - 2 < ITEMS:
                 quantise(slot - 2)
             if 0 <= slot - 1 < ITEMS:

@@ -1,3 +1,5 @@
+from contextlib import ExitStack
+
 from concourse import mybir
 from concourse.masks import make_identity
 
@@ -10,6 +12,7 @@ U8 = mybir.dt.uint8
 FP8X4 = mybir.dt.float8_e4m3fn_x4
 ACT = mybir.ActivationFunctionType
 ALU = mybir.AluOpType
+AX = mybir.AxisListType
 
 P = 128
 D = 512
@@ -20,6 +23,7 @@ S_TILES = 4
 RO_TILES = 16
 S_ITEMS = S_TILES * HALVES
 ITEMS = (S_TILES + RO_TILES) * HALVES
+VECTOR_SQUARES = {0: 2, 1: 1}
 AHEAD = 4
 
 
@@ -28,8 +32,9 @@ def tile_multiheaddistance_kernel(tc, batch_s, batch_ro, out):
     out_view = out.rearrange("(n p) m -> p n m", p=P)
 
     with (
+        ExitStack() as pinned,
         tc.tile_pool(name="const", bufs=1) as const,
-        tc.tile_pool(name="raw_pool", bufs=AHEAD + 2) as raw_pool,
+        tc.tile_pool(name="raw_pool", bufs=AHEAD + 4) as raw_pool,
         tc.tile_pool(name="work", bufs=2) as work,
         tc.tile_pool(name="deep", bufs=3) as deep,
         tc.tile_pool(name="stats", bufs=4) as stats,
@@ -46,9 +51,13 @@ def tile_multiheaddistance_kernel(tc, batch_s, batch_ro, out):
         s_codes = const.tile([P, S_ITEMS, HEADS * P], U32, align_bytes=64)
         s_scales = const.tile([P, S_ITEMS, HEADS * P], U8, align_bytes=64)
 
+        squares_v = const.tile([P, WIDTH], BF16)
+
         raw = {}
+        squares = {}
         sumsq = {}
         inv_norm = {}
+        unit = {}
         flipped = {}
         grouped = {}
         codes = {}
@@ -65,17 +74,27 @@ def tile_multiheaddistance_kernel(tc, batch_s, batch_ro, out):
                 m = tile_index - S_TILES
                 rows = batch_ro[m * P : (m + 1) * P, cols]
             raw[q] = raw_pool.tile([P, WIDTH], BF16, name="raw")
-            nc.sync.dma_start(out=raw[q][:], in_=rows)
+            pieces = HEADS if q == 0 else 1
+            for i in range(pieces):
+                part = slice(i * WIDTH // pieces, (i + 1) * WIDTH // pieces)
+                nc.sync.dma_start(out=raw[q][:, part], in_=rows[:, part])
 
-        def sum_squares(q):
-            squares = work.tile([P, WIDTH], BF16, name="squares")
+        def open_squares(q):
+            squares[q] = work.tile([P, WIDTH], BF16, name="squares")
             sumsq[q] = stats.tile([P, HEADS], F32, name="sumsq")
-            for h in range(HEADS):
-                head = slice(h * D, (h + 1) * D)
-                nc.scalar.activation(
-                    out=squares[:, head], in_=raw[q][:, head], func=ACT.Square,
-                    accum_out=sumsq[q][:, h : h + 1],
+
+        def sum_squares(q, h):
+            head = slice(h * D, (h + 1) * D)
+            if h >= HEADS - VECTOR_SQUARES.get(q, 0):
+                nc.vector.scalar_tensor_tensor(
+                    out=squares_v[:, head], in0=raw[q][:, head], scalar=1.0, in1=raw[q][:, head],
+                    op0=ALU.mult, op1=ALU.mult, accum_out=sumsq[q][:, h : h + 1],
                 )
+                return
+            nc.scalar.activation(
+                out=squares[q][:, head], in_=raw[q][:, head], func=ACT.Square,
+                accum_out=sumsq[q][:, h : h + 1],
+            )
 
         def invert_root(q):
             inv_norm[q] = stats.tile([P, HEADS], F32, name="inv_norm")
@@ -83,36 +102,36 @@ def tile_multiheaddistance_kernel(tc, batch_s, batch_ro, out):
                 out=inv_norm[q][:], in_=sumsq[q][:], func=ACT.Abs_reciprocal_sqrt
             )
 
-        def scale_and_flip(q):
-            unit = work.tile([P, WIDTH], BF16, name="unit")
-            for h in range(HEADS):
-                head = slice(h * D, (h + 1) * D)
-                nc.vector.tensor_scalar(
-                    out=unit[:, head], in0=raw[q][:, head], scalar1=inv_norm[q][:, h : h + 1],
-                    scalar2=None, op0=ALU.mult,
-                )
-            unit_words = unit[:].bitcast(F32)
+        def open_unit(q):
+            unit[q] = work.tile([P, WIDTH], BF16, name="unit")
             flipped[q] = []
-            for b in range(HEADS // 2):
-                bank = psum_t.tile([P, 2, 2, P], F32, name="bank")
-                for hh in range(2):
-                    for u in range(2):
-                        first = ((2 * b + hh) * 2 + u) * P
-                        nc.tensor.transpose(
-                            bank[:, hh, u, :], unit_words[:, first : first + P], ident[:]
-                        )
-                flipped[q].append(bank)
 
-        def regroup(q, vector_is_free):
-            grouped[q] = deep.tile([P, WIDTH], BF16, name="grouped", align_bytes=64)
+        def scale(q, h):
+            head = slice(h * D, (h + 1) * D)
+            nc.vector.tensor_scalar(
+                out=unit[q][:, head], in0=raw[q][:, head], scalar1=inv_norm[q][:, h : h + 1],
+                scalar2=None, op0=ALU.mult,
+            )
+
+        def flip(q, b):
+            unit_words = unit[q][:].bitcast(F32)
+            bank = psum_t.tile([P, 2, 2, P], F32, name="bank")
+            for hh in range(2):
+                for u in range(2):
+                    first = ((2 * b + hh) * 2 + u) * P
+                    nc.tensor.transpose(
+                        bank[:, hh, u, :], unit_words[:, first : first + P], ident[:]
+                    )
+            flipped[q].append(bank)
+
+        def regroup(q, b, engine_copy):
+            if b == 0:
+                grouped[q] = deep.tile([P, WIDTH], BF16, name="grouped", align_bytes=64)
             words = grouped[q][:].bitcast(F32).rearrange("p (h r u) -> p h r u", h=HEADS, u=2)
-            for b in range(HEADS // 2):
-                dst = words[:, 2 * b : 2 * b + 2, :, :]
-                src = flipped[q][b][:].rearrange("p h u r -> p h r u")
-                if vector_is_free:
-                    nc.vector.tensor_copy(out=dst, in_=src)
-                else:
-                    nc.scalar.copy(out=dst, in_=src)
+            engine_copy(
+                out=words[:, 2 * b : 2 * b + 2, :, :],
+                in_=flipped[q][b][:].rearrange("p h u r -> p h r u"),
+            )
 
         def quantise(q):
             if q < S_ITEMS:
@@ -127,58 +146,109 @@ def tile_multiheaddistance_kernel(tc, batch_s, batch_ro, out):
                 out=codes[q].bitcast(FP8X4), scales=scales[q], in_=grouped[q][:]
             )
 
-        def products(q):
+        def product(q, out_ap, n, h):
             half = q % HALVES
-            dist[q] = []
-            for h in range(HEADS):
-                cols = slice(h * P, (h + 1) * P)
-                bank = psum_mx.tile([P, S_TILES, P], F32, name="dist_bank")
-                for n in range(S_TILES):
-                    nc.tensor.matmul_mx(
-                        out=bank[:, n, :],
-                        lhsT=s_codes[:, n * HALVES + half, cols].bitcast(FP8X4),
-                        lhsT_scale=s_scales[:, n * HALVES + half, cols],
-                        rhs=codes[q][:, cols].bitcast(FP8X4),
-                        rhs_scale=scales[q][:, cols],
-                        start=True,
-                        stop=True,
-                    )
-                dist[q].append(bank)
+            cols = slice(h * P, (h + 1) * P)
+            nc.tensor.matmul_mx(
+                out=out_ap,
+                lhsT=s_codes[:, n * HALVES + half, cols].bitcast(FP8X4),
+                lhsT_scale=s_scales[:, n * HALVES + half, cols],
+                rhs=codes[q][:, cols].bitcast(FP8X4),
+                rhs_scale=scales[q][:, cols],
+                start=True,
+                stop=True,
+            )
 
-        def reduce_heads(q):
+        def products(q, b):
+            bank = psum_mx.tile([P, 4, P], F32, name="dist_bank")
+            dist[q, b] = bank
+            for i in range(4):
+                if q % HALVES == 0:
+                    product(q, bank[:, i, :], b, i)
+                else:
+                    product(q, bank[:, i, :], i, b)
+
+        def reduce_heads(q, b, parts=(slice(0, S_TILES),)):
             tile_index, half = divmod(q, HALVES)
             m = tile_index - S_TILES
             if half == 0:
-                best[m] = deep.tile([P, S_TILES, P], F32, name="best")
-            for h in range(HEADS):
-                for n in range(S_TILES):
-                    if half == 0 and h == 0:
-                        nc.vector.tensor_copy(out=best[m][:, n, :], in_=dist[q][h][:, n, :])
-                    else:
-                        nc.vector.tensor_tensor(
-                            out=best[m][:, n, :], in0=dist[q][h][:, n, :],
-                            in1=best[m][:, n, :], op=ALU.max,
-                        )
-            if half == HALVES - 1:
-                nc.sync.dma_start(out=out_view[:, :, m * P : (m + 1) * P], in_=best[m][:])
+                if b == 0:
+                    best[m] = deep.tile([P, S_TILES, P], F32, name="best")
+                nc.vector.tensor_reduce(
+                    out=best[m][:, b, :], in_=dist[q, b][:].rearrange("p h r -> p r h"),
+                    op=ALU.max, axis=AX.X,
+                )
+            else:
+                for part in parts:
+                    nc.vector.tensor_tensor(
+                        out=best[m][:, part, :], in0=dist[q, b][:, part, :],
+                        in1=best[m][:, part, :], op=ALU.max,
+                    )
+                if b == HEADS - 1:
+                    nc.sync.dma_start(out=out_view[:, :, m * P : (m + 1) * P], in_=best[m][:])
 
         for q in range(AHEAD):
             load(q)
-        for slot in range(ITEMS + 3):
-            reducing = S_ITEMS <= slot - 3 < ITEMS
-            if slot + AHEAD < ITEMS:
-                load(slot + AHEAD)
-            if 0 <= slot - 2 < ITEMS:
-                regroup(slot - 2, vector_is_free=not reducing)
-            if 0 <= slot - 1 < ITEMS:
-                invert_root(slot - 1)
-            if slot < ITEMS:
-                sum_squares(slot)
-            if 0 <= slot - 2 < ITEMS:
-                quantise(slot - 2)
-            if 0 <= slot - 1 < ITEMS:
-                scale_and_flip(slot - 1)
-            if reducing:
-                reduce_heads(slot - 3)
-            if S_ITEMS <= slot - 2 < ITEMS:
-                products(slot - 2)
+        pinned.enter_context(tc.manual_schedule())
+        for slot in range(ITEMS + 4):
+            new, scaled, turned, reduced = slot, slot - 2, slot - 3, slot - 4
+            is_new = new < ITEMS
+            is_scaled = 0 <= scaled < ITEMS
+            is_turned = 0 <= turned < ITEMS
+            is_multiplied = S_ITEMS <= turned < ITEMS
+            is_reduced = S_ITEMS <= reduced < ITEMS
+            by_vector = turned < S_ITEMS
+            if new + AHEAD < ITEMS:
+                load(new + AHEAD)
+            if is_new and VECTOR_SQUARES.get(new, 0):
+                open_squares(new)
+                for h in range(HEADS - VECTOR_SQUARES[new], HEADS):
+                    sum_squares(new, h)
+            if is_turned:
+                regroup(turned, 0, nc.vector.tensor_copy if by_vector else nc.scalar.copy)
+            if is_scaled:
+                open_unit(scaled)
+                scale(scaled, 0)
+                scale(scaled, 1)
+                flip(scaled, 0)
+            if is_turned:
+                last = turned == ITEMS - 1
+                regroup(turned, 1, nc.vector.tensor_copy if by_vector or last else nc.scalar.copy)
+            if is_reduced:
+                reduce_heads(reduced, 0)
+            if is_scaled:
+                scale(scaled, 2)
+                scale(scaled, 3)
+                flip(scaled, 1)
+            if is_reduced:
+                reduce_heads(reduced, 1)
+            if is_turned:
+                quantise(turned)
+            if is_new:
+                if not VECTOR_SQUARES.get(new, 0):
+                    open_squares(new)
+                sum_squares(new, 0)
+            if 0 <= new - 1 < ITEMS:
+                invert_root(new - 1)
+            if is_new:
+                for h in range(1, HEADS - VECTOR_SQUARES.get(new, 0)):
+                    sum_squares(new, h)
+            if is_multiplied:
+                products(turned, 0)
+                products(turned, 1)
+            if is_reduced:
+                if reduced % HALVES == 0:
+                    reduce_heads(reduced, 2)
+                    if is_multiplied:
+                        products(turned, 2)
+                    reduce_heads(reduced, 3)
+                    if is_multiplied:
+                        products(turned, 3)
+                else:
+                    for b in (2, 3):
+                        reduce_heads(reduced, b, (slice(0, 2), slice(2, 4)))
+                        if is_multiplied:
+                            products(turned, b)
+            elif is_multiplied:
+                products(turned, 2)
+                products(turned, 3)

@@ -23,7 +23,7 @@ S_TILES = 4
 RO_TILES = 16
 S_ITEMS = S_TILES * HALVES
 ITEMS = (S_TILES + RO_TILES) * HALVES
-VECTOR_SQUARES = {0: 2, 1: 1}
+VECTOR_SQUARES = {0: 2, 1: 1, 9: 1, 10: 1}
 AHEAD = 4
 
 
@@ -190,24 +190,32 @@ def tile_multiheaddistance_kernel(tc, batch_s, batch_ro, out):
         for q in range(AHEAD):
             load(q)
         pinned.enter_context(tc.manual_schedule())
-        for slot in range(ITEMS + 4):
-            new, scaled, turned, reduced = slot, slot - 2, slot - 3, slot - 4
+        whole = (slice(0, S_TILES),)
+        halves = (slice(0, S_TILES // 2), slice(S_TILES // 2, S_TILES))
+        for slot in range(ITEMS + 3):
+            new, scaled, turned, reduced = slot, slot - 1, slot - 2, slot - 3
             is_new = new < ITEMS
             is_scaled = 0 <= scaled < ITEMS
             is_turned = 0 <= turned < ITEMS
             is_multiplied = S_ITEMS <= turned < ITEMS
             is_reduced = S_ITEMS <= reduced < ITEMS
             by_vector = turned < S_ITEMS
+            parts = halves if reduced % HALVES == 1 else whole
             if new + AHEAD < ITEMS:
                 load(new + AHEAD)
-            if is_new and VECTOR_SQUARES.get(new, 0):
+            if is_new:
                 open_squares(new)
-                for h in range(HEADS - VECTOR_SQUARES[new], HEADS):
+                sum_squares(new, 0)
+                for h in range(HEADS - VECTOR_SQUARES.get(new, 0), HEADS):
                     sum_squares(new, h)
+            if is_scaled:
+                invert_root(scaled)
+                open_unit(scaled)
+            if is_reduced:
+                reduce_heads(reduced, 0, parts)
             if is_turned:
                 regroup(turned, 0, nc.vector.tensor_copy if by_vector else nc.scalar.copy)
             if is_scaled:
-                open_unit(scaled)
                 scale(scaled, 0)
                 scale(scaled, 1)
                 flip(scaled, 0)
@@ -215,40 +223,21 @@ def tile_multiheaddistance_kernel(tc, batch_s, batch_ro, out):
                 last = turned == ITEMS - 1
                 regroup(turned, 1, nc.vector.tensor_copy if by_vector or last else nc.scalar.copy)
             if is_reduced:
-                reduce_heads(reduced, 0)
+                reduce_heads(reduced, 1, whole)
             if is_scaled:
                 scale(scaled, 2)
                 scale(scaled, 3)
                 flip(scaled, 1)
-            if is_reduced:
-                reduce_heads(reduced, 1)
             if is_turned:
                 quantise(turned)
-            if is_new:
-                if not VECTOR_SQUARES.get(new, 0):
-                    open_squares(new)
-                sum_squares(new, 0)
-            if 0 <= new - 1 < ITEMS:
-                invert_root(new - 1)
             if is_new:
                 for h in range(1, HEADS - VECTOR_SQUARES.get(new, 0)):
                     sum_squares(new, h)
             if is_multiplied:
                 products(turned, 0)
                 products(turned, 1)
-            if is_reduced:
-                if reduced % HALVES == 0:
-                    reduce_heads(reduced, 2)
-                    if is_multiplied:
-                        products(turned, 2)
-                    reduce_heads(reduced, 3)
-                    if is_multiplied:
-                        products(turned, 3)
-                else:
-                    for b in (2, 3):
-                        reduce_heads(reduced, b, (slice(0, 2), slice(2, 4)))
-                        if is_multiplied:
-                            products(turned, b)
-            elif is_multiplied:
-                products(turned, 2)
-                products(turned, 3)
+            for b in (2, 3):
+                if is_reduced:
+                    reduce_heads(reduced, b, parts)
+                if is_multiplied:
+                    products(turned, b)

@@ -23,7 +23,7 @@ S_TILES = 4
 RO_TILES = 16
 S_ITEMS = S_TILES * HALVES
 ITEMS = (S_TILES + RO_TILES) * HALVES
-VECTOR_SQUARES = {0: 2, 1: 1, 9: 1, 10: 1}
+VECTOR_SQUARES = {0: 2, 1: 2, 2: 1, 10: 1}
 AHEAD = 4
 
 
@@ -37,9 +37,10 @@ def tile_multiheaddistance_kernel(tc, batch_s, batch_ro, out):
         tc.tile_pool(name="raw_pool", bufs=AHEAD + 4) as raw_pool,
         tc.tile_pool(name="work", bufs=2) as work,
         tc.tile_pool(name="deep", bufs=3) as deep,
-        tc.tile_pool(name="stats", bufs=4) as stats,
+        tc.tile_pool(name="stats", bufs=ITEMS) as stats,
+        tc.tile_pool(name="best_pool", bufs=RO_TILES) as best_pool,
         tc.psum_pool(name="psum_t", bufs=4) as psum_t,
-        tc.psum_pool(name="psum_mx", bufs=4) as psum_mx,
+        tc.psum_pool(name="psum_mx", bufs=1) as psum_mx,
     ):
         ident = const.tile([P, P], F32)
         make_identity(nc, ident[:])
@@ -103,7 +104,7 @@ def tile_multiheaddistance_kernel(tc, batch_s, batch_ro, out):
             )
 
         def open_unit(q):
-            unit[q] = work.tile([P, WIDTH], BF16, name="unit")
+            unit[q] = raw[q]
             flipped[q] = []
 
         def scale(q, h):
@@ -159,8 +160,15 @@ def tile_multiheaddistance_kernel(tc, batch_s, batch_ro, out):
                 stop=True,
             )
 
-        def products(q, b):
-            bank = psum_mx.tile([P, 4, P], F32, name="dist_bank")
+        def made_order(q):
+            return (0, 1, 2, 3) if (q // HALVES) % 2 == 0 else (1, 0, 3, 2)
+
+        def read_order(q):
+            return made_order(q // HALVES * HALVES + q % HALVES * HALVES)
+
+        def products(q, k):
+            b = made_order(q)[k]
+            bank = psum_mx.tile([P, 4, P], F32, name=f"dist_{b}")
             dist[q, b] = bank
             for i in range(4):
                 if q % HALVES == 0:
@@ -168,12 +176,13 @@ def tile_multiheaddistance_kernel(tc, batch_s, batch_ro, out):
                 else:
                     product(q, bank[:, i, :], i, b)
 
-        def reduce_heads(q, b, parts=(slice(0, S_TILES),)):
+        def reduce_heads(q, k, parts=(slice(0, S_TILES),)):
+            b = read_order(q)[k]
             tile_index, half = divmod(q, HALVES)
             m = tile_index - S_TILES
             if half == 0:
-                if b == 0:
-                    best[m] = deep.tile([P, S_TILES, P], F32, name="best")
+                if k == 0:
+                    best[m] = best_pool.tile([P, S_TILES, P], F32, name="best")
                 nc.vector.tensor_reduce(
                     out=best[m][:, b, :], in_=dist[q, b][:].rearrange("p h r -> p r h"),
                     op=ALU.max, axis=AX.X,
@@ -184,15 +193,15 @@ def tile_multiheaddistance_kernel(tc, batch_s, batch_ro, out):
                         out=best[m][:, part, :], in0=dist[q, b][:, part, :],
                         in1=best[m][:, part, :], op=ALU.max,
                     )
-                if b == HEADS - 1:
+                if k == HEADS - 1:
                     nc.sync.dma_start(out=out_view[:, :, m * P : (m + 1) * P], in_=best[m][:])
 
         for q in range(AHEAD):
             load(q)
         pinned.enter_context(tc.manual_schedule())
         whole = (slice(0, S_TILES),)
-        halves = (slice(0, S_TILES // 2), slice(S_TILES // 2, S_TILES))
-        for slot in range(ITEMS + 3):
+        halves = (slice(S_TILES // 2, S_TILES), slice(0, S_TILES // 2))
+        for slot in range(ITEMS + 4):
             new, scaled, turned, reduced = slot, slot - 1, slot - 2, slot - 3
             is_new = new < ITEMS
             is_scaled = 0 <= scaled < ITEMS
@@ -200,7 +209,8 @@ def tile_multiheaddistance_kernel(tc, batch_s, batch_ro, out):
             is_multiplied = S_ITEMS <= turned < ITEMS
             is_reduced = S_ITEMS <= reduced < ITEMS
             by_vector = turned < S_ITEMS
-            parts = halves if reduced % HALVES == 1 else whole
+            half = reduced % HALVES
+            parts = halves if half == 1 else whole
             if new + AHEAD < ITEMS:
                 load(new + AHEAD)
             if is_new:
@@ -211,8 +221,12 @@ def tile_multiheaddistance_kernel(tc, batch_s, batch_ro, out):
             if is_scaled:
                 invert_root(scaled)
                 open_unit(scaled)
-            if is_reduced:
-                reduce_heads(reduced, 0, parts)
+            if is_reduced and half == 0:
+                reduce_heads(reduced, 0)
+            if half == 0 and S_ITEMS <= reduced - 1 < ITEMS:
+                reduce_heads(reduced - 1, 3, halves if reduced == ITEMS else whole)
+                if is_reduced:
+                    products(reduced, 3)
             if is_turned:
                 regroup(turned, 0, nc.vector.tensor_copy if by_vector else nc.scalar.copy)
             if is_scaled:
@@ -220,14 +234,13 @@ def tile_multiheaddistance_kernel(tc, batch_s, batch_ro, out):
                 scale(scaled, 1)
                 flip(scaled, 0)
             if is_turned:
-                last = turned == ITEMS - 1
-                regroup(turned, 1, nc.vector.tensor_copy if by_vector or last else nc.scalar.copy)
-            if is_reduced:
-                reduce_heads(reduced, 1, whole)
+                regroup(turned, 1, nc.vector.tensor_copy if by_vector else nc.scalar.copy)
             if is_scaled:
                 scale(scaled, 2)
                 scale(scaled, 3)
                 flip(scaled, 1)
+            if is_reduced and half == 1:
+                reduce_heads(reduced, 0, halves if reduced == ITEMS - 1 else whole)
             if is_turned:
                 quantise(turned)
             if is_new:
@@ -235,9 +248,15 @@ def tile_multiheaddistance_kernel(tc, batch_s, batch_ro, out):
                     sum_squares(new, h)
             if is_multiplied:
                 products(turned, 0)
+            if is_reduced:
+                reduce_heads(reduced, 1, parts)
+            if is_multiplied:
                 products(turned, 1)
-            for b in (2, 3):
-                if is_reduced:
-                    reduce_heads(reduced, b, parts)
-                if is_multiplied:
-                    products(turned, b)
+            if is_reduced:
+                reduce_heads(reduced, 2, parts)
+            if is_multiplied:
+                products(turned, 2)
+            if is_reduced and half == 0:
+                reduce_heads(reduced, 3)
+            if is_multiplied and (half == 0 or not is_reduced):
+                products(turned, 3)

@@ -17,14 +17,17 @@ AX = mybir.AxisListType
 P = 128
 D = 512
 HEADS = 4
+BANKS = 4
 WIDTH = HEADS * D
 HALVES = 2
 S_TILES = 4
 RO_TILES = 16
 S_ITEMS = S_TILES * HALVES
 ITEMS = (S_TILES + RO_TILES) * HALVES
-VECTOR_SQUARES = {0: 2, 1: 2, 2: 1, 10: 1}
-AHEAD = 4
+AHEAD = 2
+PIECES = {0: ((0, 1), (2, 3), (1, 2), (3, 4), (4, 8)), 1: ((0, 4), (4, 8))}
+VECTOR_SQUARES = {0: 2, 1: 2, 2: 1, 11: 1}
+FIRST_RO = S_ITEMS
 
 
 def tile_multiheaddistance_kernel(tc, batch_s, batch_ro, out):
@@ -34,8 +37,8 @@ def tile_multiheaddistance_kernel(tc, batch_s, batch_ro, out):
     with (
         ExitStack() as pinned,
         tc.tile_pool(name="const", bufs=1) as const,
-        tc.tile_pool(name="raw_pool", bufs=AHEAD + 4) as raw_pool,
-        tc.tile_pool(name="work", bufs=2) as work,
+        tc.tile_pool(name="raw_pool", bufs=AHEAD + 2) as raw_pool,
+        tc.tile_pool(name="work", bufs=3) as work,
         tc.tile_pool(name="deep", bufs=3) as deep,
         tc.tile_pool(name="stats", bufs=ITEMS) as stats,
         tc.tile_pool(name="best_pool", bufs=RO_TILES) as best_pool,
@@ -51,7 +54,6 @@ def tile_multiheaddistance_kernel(tc, batch_s, batch_ro, out):
 
         s_codes = const.tile([P, S_ITEMS, HEADS * P], U32, align_bytes=64)
         s_scales = const.tile([P, S_ITEMS, HEADS * P], U8, align_bytes=64)
-
         squares_v = const.tile([P, WIDTH], BF16)
 
         raw = {}
@@ -66,32 +68,34 @@ def tile_multiheaddistance_kernel(tc, batch_s, batch_ro, out):
         dist = {}
         best = {}
 
-        def load(q):
-            tile_index, half = divmod(q, HALVES)
-            cols = slice(half * WIDTH, (half + 1) * WIDTH)
-            if q < S_ITEMS:
-                rows = batch_s[tile_index * P : (tile_index + 1) * P, cols]
+        def load(t):
+            if t < S_TILES:
+                rows = batch_s[t * P : (t + 1) * P, :]
             else:
-                m = tile_index - S_TILES
-                rows = batch_ro[m * P : (m + 1) * P, cols]
-            raw[q] = raw_pool.tile([P, WIDTH], BF16, name="raw")
-            pieces = HEADS if q == 0 else 1
-            for i in range(pieces):
-                part = slice(i * WIDTH // pieces, (i + 1) * WIDTH // pieces)
-                nc.sync.dma_start(out=raw[q][:, part], in_=rows[:, part])
+                rows = batch_ro[(t - S_TILES) * P : (t - S_TILES + 1) * P, :]
+            tile = raw_pool.tile([P, HALVES * WIDTH], BF16, name="raw")
+            for first, last in PIECES.get(t, ((0, HALVES * HEADS),)):
+                part = slice(first * D, last * D)
+                nc.sync.dma_start(out=tile[:, part], in_=rows[:, part])
+            for half in range(HALVES):
+                raw[t * HALVES + half] = tile[:, half * WIDTH : (half + 1) * WIDTH]
 
-        def open_squares(q):
+        def by_vector(q):
+            return VECTOR_SQUARES.get(q, 0)
+
+        def open_item(q):
             squares[q] = work.tile([P, WIDTH], BF16, name="squares")
             sumsq[q] = stats.tile([P, HEADS], F32, name="sumsq")
 
-        def sum_squares(q, h):
+        def square_v(q, h):
             head = slice(h * D, (h + 1) * D)
-            if h >= HEADS - VECTOR_SQUARES.get(q, 0):
-                nc.vector.scalar_tensor_tensor(
-                    out=squares_v[:, head], in0=raw[q][:, head], scalar=1.0, in1=raw[q][:, head],
-                    op0=ALU.mult, op1=ALU.mult, accum_out=sumsq[q][:, h : h + 1],
-                )
-                return
+            nc.vector.scalar_tensor_tensor(
+                out=squares_v[:, head], in0=raw[q][:, head], scalar=1.0, in1=raw[q][:, head],
+                op0=ALU.mult, op1=ALU.mult, accum_out=sumsq[q][:, h : h + 1],
+            )
+
+        def square_s(q, h):
+            head = slice(h * D, (h + 1) * D)
             nc.scalar.activation(
                 out=squares[q][:, head], in_=raw[q][:, head], func=ACT.Square,
                 accum_out=sumsq[q][:, h : h + 1],
@@ -104,7 +108,7 @@ def tile_multiheaddistance_kernel(tc, batch_s, batch_ro, out):
             )
 
         def open_unit(q):
-            unit[q] = raw[q]
+            unit[q] = work.tile([P, WIDTH], BF16, name="unit")
             flipped[q] = []
 
         def scale(q, h):
@@ -125,14 +129,16 @@ def tile_multiheaddistance_kernel(tc, batch_s, batch_ro, out):
                     )
             flipped[q].append(bank)
 
-        def regroup(q, b, engine_copy):
+        def regroup(q, b):
             if b == 0:
                 grouped[q] = deep.tile([P, WIDTH], BF16, name="grouped", align_bytes=64)
             words = grouped[q][:].bitcast(F32).rearrange("p (h r u) -> p h r u", h=HEADS, u=2)
-            engine_copy(
-                out=words[:, 2 * b : 2 * b + 2, :, :],
-                in_=flipped[q][b][:].rearrange("p h u r -> p h r u"),
-            )
+            dst = words[:, 2 * b : 2 * b + 2, :, :]
+            src = flipped[q][b][:].rearrange("p h u r -> p h r u")
+            if q <= FIRST_RO:
+                nc.vector.tensor_copy(out=dst, in_=src)
+            else:
+                nc.scalar.copy(out=dst, in_=src)
 
         def quantise(q):
             if q < S_ITEMS:
@@ -164,11 +170,11 @@ def tile_multiheaddistance_kernel(tc, batch_s, batch_ro, out):
             return (0, 1, 2, 3) if (q // HALVES) % 2 == 0 else (1, 0, 3, 2)
 
         def read_order(q):
-            return made_order(q // HALVES * HALVES + q % HALVES * HALVES)
+            return made_order(q) if q % HALVES == 0 else made_order(q + HALVES)
 
         def products(q, k):
             b = made_order(q)[k]
-            bank = psum_mx.tile([P, 4, P], F32, name=f"dist_{b}")
+            bank = psum_mx.tile([P, BANKS, P], F32, name=f"dist_{b}")
             dist[q, b] = bank
             for i in range(4):
                 if q % HALVES == 0:
@@ -193,14 +199,16 @@ def tile_multiheaddistance_kernel(tc, batch_s, batch_ro, out):
                         out=best[m][:, part, :], in0=dist[q, b][:, part, :],
                         in1=best[m][:, part, :], op=ALU.max,
                     )
-                if k == HEADS - 1:
-                    nc.sync.dma_start(out=out_view[:, :, m * P : (m + 1) * P], in_=best[m][:])
+                    if k == BANKS - 1:
+                        nc.sync.dma_start(
+                            out=out_view[:, part, m * P : (m + 1) * P], in_=best[m][:, part, :]
+                        )
 
-        for q in range(AHEAD):
-            load(q)
+        for t in range(AHEAD):
+            load(t)
         pinned.enter_context(tc.manual_schedule())
         whole = (slice(0, S_TILES),)
-        halves = (slice(S_TILES // 2, S_TILES), slice(0, S_TILES // 2))
+        halves = (slice(0, S_TILES // 2), slice(S_TILES // 2, S_TILES))
         for slot in range(ITEMS + 4):
             new, scaled, turned, reduced = slot, slot - 1, slot - 2, slot - 3
             is_new = new < ITEMS
@@ -208,16 +216,15 @@ def tile_multiheaddistance_kernel(tc, batch_s, batch_ro, out):
             is_turned = 0 <= turned < ITEMS
             is_multiplied = S_ITEMS <= turned < ITEMS
             is_reduced = S_ITEMS <= reduced < ITEMS
-            by_vector = turned < S_ITEMS
             half = reduced % HALVES
             parts = halves if half == 1 else whole
-            if new + AHEAD < ITEMS:
-                load(new + AHEAD)
+            if new % HALVES == 0 and new // HALVES + AHEAD < S_TILES + RO_TILES:
+                load(new // HALVES + AHEAD)
             if is_new:
-                open_squares(new)
-                sum_squares(new, 0)
-                for h in range(HEADS - VECTOR_SQUARES.get(new, 0), HEADS):
-                    sum_squares(new, h)
+                open_item(new)
+                square_s(new, 0)
+                for h in range(HEADS - by_vector(new), HEADS):
+                    square_v(new, h)
             if is_scaled:
                 invert_root(scaled)
                 open_unit(scaled)
@@ -228,13 +235,13 @@ def tile_multiheaddistance_kernel(tc, batch_s, batch_ro, out):
                 if is_reduced:
                     products(reduced, 3)
             if is_turned:
-                regroup(turned, 0, nc.vector.tensor_copy if by_vector else nc.scalar.copy)
+                regroup(turned, 0)
             if is_scaled:
                 scale(scaled, 0)
                 scale(scaled, 1)
                 flip(scaled, 0)
             if is_turned:
-                regroup(turned, 1, nc.vector.tensor_copy if by_vector else nc.scalar.copy)
+                regroup(turned, 1)
             if is_scaled:
                 scale(scaled, 2)
                 scale(scaled, 3)
@@ -244,8 +251,8 @@ def tile_multiheaddistance_kernel(tc, batch_s, batch_ro, out):
             if is_turned:
                 quantise(turned)
             if is_new:
-                for h in range(1, HEADS - VECTOR_SQUARES.get(new, 0)):
-                    sum_squares(new, h)
+                for h in range(1, HEADS - by_vector(new)):
+                    square_s(new, h)
             if is_multiplied:
                 products(turned, 0)
             if is_reduced:

@@ -26,8 +26,10 @@ S_ITEMS = S_TILES * HALVES
 ITEMS = (S_TILES + RO_TILES) * HALVES
 AHEAD = 2
 PIECES = {0: ((0, 1), (2, 3), (1, 2), (3, 4), (4, 8)), 1: ((0, 4), (4, 8))}
-VECTOR_SQUARES = {0: 2, 1: 2, 2: 1, 11: 1}
-FIRST_RO = S_ITEMS
+VECTOR_SQUARES = {0: 2, 1: 2}
+GP_RO = 2
+COPY_LAST = 34
+COPY_EVERY = 4
 
 
 def tile_multiheaddistance_kernel(tc, batch_s, batch_ro, out):
@@ -40,6 +42,7 @@ def tile_multiheaddistance_kernel(tc, batch_s, batch_ro, out):
         tc.tile_pool(name="raw_pool", bufs=AHEAD + 2) as raw_pool,
         tc.tile_pool(name="work", bufs=3) as work,
         tc.tile_pool(name="deep", bufs=3) as deep,
+        tc.tile_pool(name="turn_pool", bufs=1) as turn_pool,
         tc.tile_pool(name="stats", bufs=ITEMS) as stats,
         tc.tile_pool(name="best_pool", bufs=RO_TILES) as best_pool,
         tc.psum_pool(name="psum_t", bufs=4) as psum_t,
@@ -80,6 +83,9 @@ def tile_multiheaddistance_kernel(tc, batch_s, batch_ro, out):
             for half in range(HALVES):
                 raw[t * HALVES + half] = tile[:, half * WIDTH : (half + 1) * WIDTH]
 
+        def gp_heads(q):
+            return 0 if q < S_ITEMS else GP_RO
+
         def by_vector(q):
             return VECTOR_SQUARES.get(q, 0)
 
@@ -108,22 +114,35 @@ def tile_multiheaddistance_kernel(tc, batch_s, batch_ro, out):
             )
 
         def open_unit(q):
-            unit[q] = work.tile([P, WIDTH], BF16, name="unit")
+            unit[q, 0] = work.tile([P, WIDTH // 2], BF16, name="unit_0")
             flipped[q] = []
 
+        def open_gated(q):
+            if q < S_ITEMS:
+                unit[q, 1] = work.tile([P, WIDTH // 2], BF16, name="unit_1")
+            else:
+                unit[q, 1] = turn_pool.tile([P, WIDTH // 2], BF16, name=f"turn_{q % 2}", align_bytes=64)
+
         def scale(q, h):
+            unit_head = unit[q, h // 2][:, h % 2 * D : (h % 2 + 1) * D]
             head = slice(h * D, (h + 1) * D)
+            if h >= HEADS - gp_heads(q):
+                nc.gpsimd.tensor_scalar(
+                    out=unit_head, in0=raw[q][:, head], scalar1=inv_norm[q][:, h : h + 1],
+                    scalar2=1.0, op0=ALU.mult, op1=ALU.mult,
+                )
+                return
             nc.vector.tensor_scalar(
-                out=unit[q][:, head], in0=raw[q][:, head], scalar1=inv_norm[q][:, h : h + 1],
+                out=unit_head, in0=raw[q][:, head], scalar1=inv_norm[q][:, h : h + 1],
                 scalar2=None, op0=ALU.mult,
             )
 
         def flip(q, b):
-            unit_words = unit[q][:].bitcast(F32)
+            unit_words = unit[q, b][:].bitcast(F32)
             bank = psum_t.tile([P, 2, 2, P], F32, name="bank")
             for hh in range(2):
                 for u in range(2):
-                    first = ((2 * b + hh) * 2 + u) * P
+                    first = (hh * 2 + u) * P
                     nc.tensor.transpose(
                         bank[:, hh, u, :], unit_words[:, first : first + P], ident[:]
                     )
@@ -131,11 +150,14 @@ def tile_multiheaddistance_kernel(tc, batch_s, batch_ro, out):
 
         def regroup(q, b):
             if b == 0:
-                grouped[q] = deep.tile([P, WIDTH], BF16, name="grouped", align_bytes=64)
+                if q < S_ITEMS:
+                    grouped[q] = deep.tile([P, WIDTH], BF16, name="grouped", align_bytes=64)
+                else:
+                    grouped[q] = turn_pool.tile([P, WIDTH], BF16, name=f"turn_{q % 2}", align_bytes=64)
             words = grouped[q][:].bitcast(F32).rearrange("p (h r u) -> p h r u", h=HEADS, u=2)
             dst = words[:, 2 * b : 2 * b + 2, :, :]
             src = flipped[q][b][:].rearrange("p h u r -> p h r u")
-            if q <= FIRST_RO:
+            if q <= S_ITEMS or q % COPY_EVERY == 0 and b == 1 and q < COPY_LAST:
                 nc.vector.tensor_copy(out=dst, in_=src)
             else:
                 nc.scalar.copy(out=dst, in_=src)
@@ -209,11 +231,14 @@ def tile_multiheaddistance_kernel(tc, batch_s, batch_ro, out):
         pinned.enter_context(tc.manual_schedule())
         whole = (slice(0, S_TILES),)
         halves = (slice(0, S_TILES // 2), slice(S_TILES // 2, S_TILES))
-        for slot in range(ITEMS + 4):
-            new, scaled, turned, reduced = slot, slot - 1, slot - 2, slot - 3
+        for slot in range(ITEMS + 5):
+            new, scaled, reduced = slot, slot - 1, slot - 4
+            flipping = slot - 1 if slot - 1 < S_ITEMS else slot - 2
+            turned = slot - 2 if slot - 2 < S_ITEMS else slot - 3
             is_new = new < ITEMS
             is_scaled = 0 <= scaled < ITEMS
-            is_turned = 0 <= turned < ITEMS
+            is_flipped = 0 <= flipping < ITEMS and not (slot - 1 >= S_ITEMS and flipping < S_ITEMS)
+            is_turned = 0 <= turned < ITEMS and not (slot - 2 >= S_ITEMS and turned < S_ITEMS)
             is_multiplied = S_ITEMS <= turned < ITEMS
             is_reduced = S_ITEMS <= reduced < ITEMS
             half = reduced % HALVES
@@ -223,11 +248,18 @@ def tile_multiheaddistance_kernel(tc, batch_s, batch_ro, out):
             if is_new:
                 open_item(new)
                 square_s(new, 0)
+            if is_flipped and flipping >= S_ITEMS:
+                flip(flipping, 0)
+                flip(flipping, 1)
+            if is_scaled:
+                invert_root(scaled)
+            if is_new and new < S_ITEMS + 4:
                 for h in range(HEADS - by_vector(new), HEADS):
                     square_v(new, h)
             if is_scaled:
-                invert_root(scaled)
                 open_unit(scaled)
+                if scaled < S_ITEMS:
+                    open_gated(scaled)
             if is_reduced and half == 0:
                 reduce_heads(reduced, 0)
             if half == 0 and S_ITEMS <= reduced - 1 < ITEMS:
@@ -236,20 +268,33 @@ def tile_multiheaddistance_kernel(tc, batch_s, batch_ro, out):
                     products(reduced, 3)
             if is_turned:
                 regroup(turned, 0)
-            if is_scaled:
+            if is_scaled and scaled < S_ITEMS:
                 scale(scaled, 0)
                 scale(scaled, 1)
                 flip(scaled, 0)
             if is_turned:
                 regroup(turned, 1)
-            if is_scaled:
+            if is_scaled and scaled < S_ITEMS:
                 scale(scaled, 2)
                 scale(scaled, 3)
                 flip(scaled, 1)
+            if is_reduced and half == 1 and is_scaled and scaled >= S_ITEMS:
+                for h in range(HEADS - GP_RO):
+                    scale(scaled, h)
             if is_reduced and half == 1:
                 reduce_heads(reduced, 0, halves if reduced == ITEMS - 1 else whole)
+            if is_new and new >= S_ITEMS + 4:
+                for h in range(HEADS - by_vector(new), HEADS):
+                    square_v(new, h)
+            if is_scaled and scaled >= S_ITEMS and not (is_reduced and half == 1):
+                for h in range(HEADS - GP_RO):
+                    scale(scaled, h)
             if is_turned:
                 quantise(turned)
+            if is_scaled and scaled >= S_ITEMS:
+                open_gated(scaled)
+                for h in range(HEADS - GP_RO, HEADS):
+                    scale(scaled, h)
             if is_new:
                 for h in range(1, HEADS - by_vector(new)):
                     square_s(new, h)

@@ -17,19 +17,20 @@ AX = mybir.AxisListType
 P = 128
 D = 512
 HEADS = 4
-BANKS = 4
-WIDTH = HEADS * D
 HALVES = 2
+WIDTH = HEADS * D
+PAIR = 2 * D
+BANKS = 4
 S_TILES = 4
 RO_TILES = 16
 S_ITEMS = S_TILES * HALVES
 ITEMS = (S_TILES + RO_TILES) * HALVES
+
 AHEAD = 2
 PIECES = {0: ((0, 1), (2, 3), (1, 2), (3, 4), (4, 8)), 1: ((0, 4), (4, 8))}
-VECTOR_SQUARES = {0: 2, 1: 2}
-GP_RO = 2
-COPY_LAST = 34
-COPY_EVERY = 4
+VECTOR_SQUARES = {0: 2, 1: 2, 2: 1, 12: 1}
+GPSIMD_FROM = S_ITEMS + 2
+VECTOR_COPIES = range(14, 34, 4)
 
 
 def tile_multiheaddistance_kernel(tc, batch_s, batch_ro, out):
@@ -57,7 +58,7 @@ def tile_multiheaddistance_kernel(tc, batch_s, batch_ro, out):
 
         s_codes = const.tile([P, S_ITEMS, HEADS * P], U32, align_bytes=64)
         s_scales = const.tile([P, S_ITEMS, HEADS * P], U8, align_bytes=64)
-        squares_v = const.tile([P, WIDTH], BF16)
+        vector_squares = const.tile([P, WIDTH], BF16)
 
         raw = {}
         squares = {}
@@ -77,33 +78,31 @@ def tile_multiheaddistance_kernel(tc, batch_s, batch_ro, out):
             else:
                 rows = batch_ro[(t - S_TILES) * P : (t - S_TILES + 1) * P, :]
             tile = raw_pool.tile([P, HALVES * WIDTH], BF16, name="raw")
-            for first, last in PIECES.get(t, ((0, HALVES * HEADS),)):
-                part = slice(first * D, last * D)
+            for first, end in PIECES.get(t, ((0, HALVES * HEADS),)):
+                part = slice(first * D, end * D)
                 nc.sync.dma_start(out=tile[:, part], in_=rows[:, part])
             for half in range(HALVES):
                 raw[t * HALVES + half] = tile[:, half * WIDTH : (half + 1) * WIDTH]
-
-        def gp_heads(q):
-            return 0 if q < S_ITEMS else GP_RO
-
-        def by_vector(q):
-            return VECTOR_SQUARES.get(q, 0)
 
         def open_item(q):
             squares[q] = work.tile([P, WIDTH], BF16, name="squares")
             sumsq[q] = stats.tile([P, HEADS], F32, name="sumsq")
 
-        def square_v(q, h):
-            head = slice(h * D, (h + 1) * D)
-            nc.vector.scalar_tensor_tensor(
-                out=squares_v[:, head], in0=raw[q][:, head], scalar=1.0, in1=raw[q][:, head],
-                op0=ALU.mult, op1=ALU.mult, accum_out=sumsq[q][:, h : h + 1],
-            )
+        def scalar_heads(q):
+            return HEADS - VECTOR_SQUARES.get(q, 0)
 
-        def square_s(q, h):
+        def square_on_scalar(q, h):
             head = slice(h * D, (h + 1) * D)
             nc.scalar.activation(
                 out=squares[q][:, head], in_=raw[q][:, head], func=ACT.Square,
+                accum_out=sumsq[q][:, h : h + 1],
+            )
+
+        def square_on_vector(q, h):
+            head = slice(h * D, (h + 1) * D)
+            nc.vector.scalar_tensor_tensor(
+                out=vector_squares[:, head], in0=raw[q][:, head], scalar=1.0,
+                in1=raw[q][:, head], op0=ALU.mult, op1=ALU.mult,
                 accum_out=sumsq[q][:, h : h + 1],
             )
 
@@ -113,51 +112,54 @@ def tile_multiheaddistance_kernel(tc, batch_s, batch_ro, out):
                 out=inv_norm[q][:], in_=sumsq[q][:], func=ACT.Abs_reciprocal_sqrt
             )
 
-        def open_unit(q):
-            unit[q, 0] = work.tile([P, WIDTH // 2], BF16, name="unit_0")
+        def open_first_pair(q):
+            unit[q, 0] = work.tile([P, PAIR], BF16, name="unit_0")
             flipped[q] = []
 
-        def open_gated(q):
+        def open_second_pair(q):
             if q < S_ITEMS:
-                unit[q, 1] = work.tile([P, WIDTH // 2], BF16, name="unit_1")
+                unit[q, 1] = work.tile([P, PAIR], BF16, name="unit_1")
             else:
-                unit[q, 1] = turn_pool.tile([P, WIDTH // 2], BF16, name=f"turn_{q % 2}", align_bytes=64)
+                unit[q, 1] = turn_pool.tile([P, PAIR], BF16, name=f"turn_{q % 2}", align_bytes=64)
 
-        def scale(q, h):
-            unit_head = unit[q, h // 2][:, h % 2 * D : (h % 2 + 1) * D]
-            head = slice(h * D, (h + 1) * D)
-            if h >= HEADS - gp_heads(q):
-                nc.gpsimd.tensor_scalar(
-                    out=unit_head, in0=raw[q][:, head], scalar1=inv_norm[q][:, h : h + 1],
-                    scalar2=1.0, op0=ALU.mult, op1=ALU.mult,
-                )
-                return
-            nc.vector.tensor_scalar(
-                out=unit_head, in0=raw[q][:, head], scalar1=inv_norm[q][:, h : h + 1],
-                scalar2=None, op0=ALU.mult,
-            )
+        def scale_pair(q, pair):
+            for hh in range(2):
+                h = 2 * pair + hh
+                dst = unit[q, pair][:, hh * D : (hh + 1) * D]
+                src = raw[q][:, h * D : (h + 1) * D]
+                factor = inv_norm[q][:, h : h + 1]
+                if pair == 1 and q >= GPSIMD_FROM:
+                    nc.gpsimd.tensor_scalar(
+                        out=dst, in0=src, scalar1=factor, scalar2=1.0, op0=ALU.mult, op1=ALU.mult
+                    )
+                elif q == ITEMS - 1:
+                    nc.scalar.activation(out=dst, in_=src, func=ACT.Copy, scale=factor)
+                else:
+                    nc.vector.tensor_scalar(
+                        out=dst, in0=src, scalar1=factor, scalar2=None, op0=ALU.mult
+                    )
 
-        def flip(q, b):
-            unit_words = unit[q, b][:].bitcast(F32)
+        def flip(q, pair):
+            words = unit[q, pair][:].bitcast(F32)
             bank = psum_t.tile([P, 2, 2, P], F32, name="bank")
             for hh in range(2):
                 for u in range(2):
                     first = (hh * 2 + u) * P
-                    nc.tensor.transpose(
-                        bank[:, hh, u, :], unit_words[:, first : first + P], ident[:]
-                    )
+                    nc.tensor.transpose(bank[:, hh, u, :], words[:, first : first + P], ident[:])
             flipped[q].append(bank)
 
-        def regroup(q, b):
-            if b == 0:
+        def regroup(q, pair):
+            if pair == 0:
                 if q < S_ITEMS:
                     grouped[q] = deep.tile([P, WIDTH], BF16, name="grouped", align_bytes=64)
                 else:
-                    grouped[q] = turn_pool.tile([P, WIDTH], BF16, name=f"turn_{q % 2}", align_bytes=64)
+                    grouped[q] = turn_pool.tile(
+                        [P, WIDTH], BF16, name=f"turn_{q % 2}", align_bytes=64
+                    )
             words = grouped[q][:].bitcast(F32).rearrange("p (h r u) -> p h r u", h=HEADS, u=2)
-            dst = words[:, 2 * b : 2 * b + 2, :, :]
-            src = flipped[q][b][:].rearrange("p h u r -> p h r u")
-            if q <= S_ITEMS or q % COPY_EVERY == 0 and b == 1 and q < COPY_LAST:
+            dst = words[:, 2 * pair : 2 * pair + 2, :, :]
+            src = flipped[q][pair][:].rearrange("p h u r -> p h r u")
+            if q <= S_ITEMS or (pair == 1 and q in VECTOR_COPIES):
                 nc.vector.tensor_copy(out=dst, in_=src)
             else:
                 nc.scalar.copy(out=dst, in_=src)
@@ -176,12 +178,12 @@ def tile_multiheaddistance_kernel(tc, batch_s, batch_ro, out):
             )
 
         def product(q, out_ap, n, h):
-            half = q % HALVES
+            s_item = n * HALVES + q % HALVES
             cols = slice(h * P, (h + 1) * P)
             nc.tensor.matmul_mx(
                 out=out_ap,
-                lhsT=s_codes[:, n * HALVES + half, cols].bitcast(FP8X4),
-                lhsT_scale=s_scales[:, n * HALVES + half, cols],
+                lhsT=s_codes[:, s_item, cols].bitcast(FP8X4),
+                lhsT_scale=s_scales[:, s_item, cols],
                 rhs=codes[q][:, cols].bitcast(FP8X4),
                 rhs_scale=scales[q][:, cols],
                 start=True,
@@ -196,7 +198,7 @@ def tile_multiheaddistance_kernel(tc, batch_s, batch_ro, out):
 
         def products(q, k):
             b = made_order(q)[k]
-            bank = psum_mx.tile([P, BANKS, P], F32, name=f"dist_{b}")
+            bank = psum_mx.tile([P, 4, P], F32, name=f"dist_{b}")
             dist[q, b] = bank
             for i in range(4):
                 if q % HALVES == 0:
@@ -204,111 +206,102 @@ def tile_multiheaddistance_kernel(tc, batch_s, batch_ro, out):
                 else:
                     product(q, bank[:, i, :], i, b)
 
-        def reduce_heads(q, k, parts=(slice(0, S_TILES),)):
+        def reduce_bank(q, k):
             b = read_order(q)[k]
-            tile_index, half = divmod(q, HALVES)
-            m = tile_index - S_TILES
-            if half == 0:
-                if k == 0:
-                    best[m] = best_pool.tile([P, S_TILES, P], F32, name="best")
-                nc.vector.tensor_reduce(
-                    out=best[m][:, b, :], in_=dist[q, b][:].rearrange("p h r -> p r h"),
-                    op=ALU.max, axis=AX.X,
+            m = q // HALVES - S_TILES
+            if k == 0:
+                best[m] = best_pool.tile([P, S_TILES, P], F32, name="best")
+            nc.vector.tensor_reduce(
+                out=best[m][:, b, :], in_=dist[q, b][:].rearrange("p h r -> p r h"),
+                op=ALU.max, axis=AX.X,
+            )
+
+        def link_bank(q, k, parts):
+            b = read_order(q)[k]
+            m = q // HALVES - S_TILES
+            for part in parts:
+                nc.vector.tensor_tensor(
+                    out=best[m][:, part, :], in0=dist[q, b][:, part, :],
+                    in1=best[m][:, part, :], op=ALU.max,
                 )
-            else:
-                for part in parts:
-                    nc.vector.tensor_tensor(
-                        out=best[m][:, part, :], in0=dist[q, b][:, part, :],
-                        in1=best[m][:, part, :], op=ALU.max,
+                if k == BANKS - 1:
+                    nc.sync.dma_start(
+                        out=out_view[:, part, m * P : (m + 1) * P], in_=best[m][:, part, :]
                     )
-                    if k == BANKS - 1:
-                        nc.sync.dma_start(
-                            out=out_view[:, part, m * P : (m + 1) * P], in_=best[m][:, part, :]
-                        )
+
+        whole = (slice(0, S_TILES),)
+        halves = (slice(0, S_TILES // 2), slice(S_TILES // 2, S_TILES))
 
         for t in range(AHEAD):
             load(t)
         pinned.enter_context(tc.manual_schedule())
-        whole = (slice(0, S_TILES),)
-        halves = (slice(0, S_TILES // 2), slice(S_TILES // 2, S_TILES))
         for slot in range(ITEMS + 5):
-            new, scaled, reduced = slot, slot - 1, slot - 4
-            flipping = slot - 1 if slot - 1 < S_ITEMS else slot - 2
+            new = slot
+            scaled = slot - 1
+            flipping = slot - 2
             turned = slot - 2 if slot - 2 < S_ITEMS else slot - 3
+            reduced = slot - 4
             is_new = new < ITEMS
-            is_scaled = 0 <= scaled < ITEMS
-            is_flipped = 0 <= flipping < ITEMS and not (slot - 1 >= S_ITEMS and flipping < S_ITEMS)
-            is_turned = 0 <= turned < ITEMS and not (slot - 2 >= S_ITEMS and turned < S_ITEMS)
-            is_multiplied = S_ITEMS <= turned < ITEMS
+            is_scaled = scaled < ITEMS and slot >= 1
+            is_short = is_scaled and scaled < S_ITEMS
+            is_long = is_scaled and scaled >= S_ITEMS
+            is_flipped = S_ITEMS <= flipping < ITEMS
+            is_turned = 0 <= turned < ITEMS and slot != S_ITEMS + 2
+            is_multiplied = is_turned and turned >= S_ITEMS
             is_reduced = S_ITEMS <= reduced < ITEMS
             half = reduced % HALVES
-            parts = halves if half == 1 else whole
             if new % HALVES == 0 and new // HALVES + AHEAD < S_TILES + RO_TILES:
                 load(new // HALVES + AHEAD)
             if is_new:
                 open_item(new)
-                square_s(new, 0)
-            if is_flipped and flipping >= S_ITEMS:
+                square_on_scalar(new, 0)
+            if is_flipped:
                 flip(flipping, 0)
                 flip(flipping, 1)
             if is_scaled:
                 invert_root(scaled)
-            if is_new and new < S_ITEMS + 4:
-                for h in range(HEADS - by_vector(new), HEADS):
-                    square_v(new, h)
-            if is_scaled:
-                open_unit(scaled)
-                if scaled < S_ITEMS:
-                    open_gated(scaled)
+                open_first_pair(scaled)
+            if is_new:
+                for h in range(scalar_heads(new), HEADS):
+                    square_on_vector(new, h)
             if is_reduced and half == 0:
-                reduce_heads(reduced, 0)
-            if half == 0 and S_ITEMS <= reduced - 1 < ITEMS:
-                reduce_heads(reduced - 1, 3, halves if reduced == ITEMS else whole)
-                if is_reduced:
-                    products(reduced, 3)
+                reduce_bank(reduced, 0)
+            if half == 0 and S_ITEMS < reduced <= ITEMS:
+                link_bank(reduced - 1, 3, halves if reduced == ITEMS else whole)
+            if is_reduced and half == 0:
+                products(reduced, 3)
             if is_turned:
                 regroup(turned, 0)
-            if is_scaled and scaled < S_ITEMS:
-                scale(scaled, 0)
-                scale(scaled, 1)
+            if is_short:
+                scale_pair(scaled, 0)
                 flip(scaled, 0)
             if is_turned:
                 regroup(turned, 1)
-            if is_scaled and scaled < S_ITEMS:
-                scale(scaled, 2)
-                scale(scaled, 3)
+            if is_short:
+                open_second_pair(scaled)
+                scale_pair(scaled, 1)
                 flip(scaled, 1)
-            if is_reduced and half == 1 and is_scaled and scaled >= S_ITEMS:
-                for h in range(HEADS - GP_RO):
-                    scale(scaled, h)
+            if is_long:
+                scale_pair(scaled, 0)
             if is_reduced and half == 1:
-                reduce_heads(reduced, 0, halves if reduced == ITEMS - 1 else whole)
-            if is_new and new >= S_ITEMS + 4:
-                for h in range(HEADS - by_vector(new), HEADS):
-                    square_v(new, h)
-            if is_scaled and scaled >= S_ITEMS and not (is_reduced and half == 1):
-                for h in range(HEADS - GP_RO):
-                    scale(scaled, h)
+                link_bank(reduced, 0, halves if reduced == ITEMS - 1 else whole)
             if is_turned:
                 quantise(turned)
-            if is_scaled and scaled >= S_ITEMS:
-                open_gated(scaled)
-                for h in range(HEADS - GP_RO, HEADS):
-                    scale(scaled, h)
+            if is_long:
+                open_second_pair(scaled)
+                scale_pair(scaled, 1)
             if is_new:
-                for h in range(1, HEADS - by_vector(new)):
-                    square_s(new, h)
-            if is_multiplied:
-                products(turned, 0)
-            if is_reduced:
-                reduce_heads(reduced, 1, parts)
-            if is_multiplied:
-                products(turned, 1)
-            if is_reduced:
-                reduce_heads(reduced, 2, parts)
-            if is_multiplied:
-                products(turned, 2)
+                for h in range(1, scalar_heads(new)):
+                    square_on_scalar(new, h)
+            for k in range(3):
+                if is_multiplied:
+                    products(turned, k)
+                if is_reduced and k < 2:
+                    if half == 0:
+                        reduce_bank(reduced, k + 1)
+                    else:
+                        link_bank(reduced, k + 1, halves)
             if is_reduced and half == 0:
-                reduce_heads(reduced, 3)
-            if is_multiplied and (half == 0 or not is_reduced):
+                reduce_bank(reduced, 3)
+            if is_multiplied and turned % HALVES == 1:
                 products(turned, 3)

from contextlib import ExitStack

from concourse import mybir
from concourse.masks import make_identity

FLOPS = 2 * 512 * 2048 * 4096

BF16 = mybir.dt.bfloat16
F32 = mybir.dt.float32
U32 = mybir.dt.uint32
U8 = mybir.dt.uint8
FP8X4 = mybir.dt.float8_e4m3fn_x4
ACT = mybir.ActivationFunctionType
ALU = mybir.AluOpType
AX = mybir.AxisListType

P = 128
D = 512
HEADS = 4
HALVES = 2
WIDTH = HEADS * D
PAIR = 2 * D
BANKS = 4
S_TILES = 4
RO_TILES = 16
S_ITEMS = S_TILES * HALVES
ITEMS = (S_TILES + RO_TILES) * HALVES

AHEAD = 2
PIECES = {0: ((0, 1), (2, 3), (1, 2), (3, 4), (4, 8)), 1: ((0, 4), (4, 8))}
VECTOR_SQUARES = {0: 2, 1: 2, 2: 1, 12: 1}
GPSIMD_FROM = S_ITEMS + 2
VECTOR_COPIES = range(14, 34, 4)


def tile_multiheaddistance_kernel(tc, batch_s, batch_ro, out):
    nc = tc.nc
    out_view = out.rearrange("(n p) m -> p n m", p=P)

    with (
        ExitStack() as pinned,
        tc.tile_pool(name="const", bufs=1) as const,
        tc.tile_pool(name="raw_pool", bufs=AHEAD + 2) as raw_pool,
        tc.tile_pool(name="work", bufs=3) as work,
        tc.tile_pool(name="deep", bufs=3) as deep,
        tc.tile_pool(name="turn_pool", bufs=1) as turn_pool,
        tc.tile_pool(name="stats", bufs=ITEMS) as stats,
        tc.tile_pool(name="best_pool", bufs=RO_TILES) as best_pool,
        tc.psum_pool(name="psum_t", bufs=4) as psum_t,
        tc.psum_pool(name="psum_mx", bufs=1) as psum_mx,
    ):
        ident = const.tile([P, P], F32)
        make_identity(nc, ident[:])
        one = const.tile([P, 1], F32)
        nc.vector.memset(one[:], 1.0)
        warm = const.tile([P, 1], F32)
        nc.scalar.activation(out=warm[:], in_=one[:], func=ACT.Abs_reciprocal_sqrt)

        s_codes = const.tile([P, S_ITEMS, HEADS * P], U32, align_bytes=64)
        s_scales = const.tile([P, S_ITEMS, HEADS * P], U8, align_bytes=64)
        vector_squares = const.tile([P, WIDTH], BF16)

        raw = {}
        squares = {}
        sumsq = {}
        inv_norm = {}
        unit = {}
        flipped = {}
        grouped = {}
        codes = {}
        scales = {}
        dist = {}
        best = {}

        def load(t):
            if t < S_TILES:
                rows = batch_s[t * P : (t + 1) * P, :]
            else:
                rows = batch_ro[(t - S_TILES) * P : (t - S_TILES + 1) * P, :]
            tile = raw_pool.tile([P, HALVES * WIDTH], BF16, name="raw")
            for first, end in PIECES.get(t, ((0, HALVES * HEADS),)):
                part = slice(first * D, end * D)
                nc.sync.dma_start(out=tile[:, part], in_=rows[:, part])
            for half in range(HALVES):
                raw[t * HALVES + half] = tile[:, half * WIDTH : (half + 1) * WIDTH]

        def open_item(q):
            squares[q] = work.tile([P, WIDTH], BF16, name="squares")
            sumsq[q] = stats.tile([P, HEADS], F32, name="sumsq")

        def scalar_heads(q):
            return HEADS - VECTOR_SQUARES.get(q, 0)

        def square_on_scalar(q, h):
            head = slice(h * D, (h + 1) * D)
            nc.scalar.activation(
                out=squares[q][:, head], in_=raw[q][:, head], func=ACT.Square,
                accum_out=sumsq[q][:, h : h + 1],
            )

        def square_on_vector(q, h):
            head = slice(h * D, (h + 1) * D)
            nc.vector.scalar_tensor_tensor(
                out=vector_squares[:, head], in0=raw[q][:, head], scalar=1.0,
                in1=raw[q][:, head], op0=ALU.mult, op1=ALU.mult,
                accum_out=sumsq[q][:, h : h + 1],
            )

        def invert_root(q):
            inv_norm[q] = stats.tile([P, HEADS], F32, name="inv_norm")
            nc.scalar.activation(
                out=inv_norm[q][:], in_=sumsq[q][:], func=ACT.Abs_reciprocal_sqrt
            )

        def open_first_pair(q):
            unit[q, 0] = work.tile([P, PAIR], BF16, name="unit_0")
            flipped[q] = []

        def open_second_pair(q):
            if q < S_ITEMS:
                unit[q, 1] = work.tile([P, PAIR], BF16, name="unit_1")
            else:
                unit[q, 1] = turn_pool.tile([P, PAIR], BF16, name=f"turn_{q % 2}", align_bytes=64)

        def scale_pair(q, pair):
            for hh in range(2):
                h = 2 * pair + hh
                dst = unit[q, pair][:, hh * D : (hh + 1) * D]
                src = raw[q][:, h * D : (h + 1) * D]
                factor = inv_norm[q][:, h : h + 1]
                if pair == 1 and q >= GPSIMD_FROM:
                    nc.gpsimd.tensor_scalar(
                        out=dst, in0=src, scalar1=factor, scalar2=1.0, op0=ALU.mult, op1=ALU.mult
                    )
                elif q == ITEMS - 1:
                    nc.scalar.activation(out=dst, in_=src, func=ACT.Copy, scale=factor)
                else:
                    nc.vector.tensor_scalar(
                        out=dst, in0=src, scalar1=factor, scalar2=None, op0=ALU.mult
                    )

        def flip(q, pair):
            words = unit[q, pair][:].bitcast(F32)
            bank = psum_t.tile([P, 2, 2, P], F32, name="bank")
            for hh in range(2):
                for u in range(2):
                    first = (hh * 2 + u) * P
                    nc.tensor.transpose(bank[:, hh, u, :], words[:, first : first + P], ident[:])
            flipped[q].append(bank)

        def regroup(q, pair):
            if pair == 0:
                if q < S_ITEMS:
                    grouped[q] = deep.tile([P, WIDTH], BF16, name="grouped", align_bytes=64)
                else:
                    grouped[q] = turn_pool.tile(
                        [P, WIDTH], BF16, name=f"turn_{q % 2}", align_bytes=64
                    )
            words = grouped[q][:].bitcast(F32).rearrange("p (h r u) -> p h r u", h=HEADS, u=2)
            dst = words[:, 2 * pair : 2 * pair + 2, :, :]
            src = flipped[q][pair][:].rearrange("p h u r -> p h r u")
            if q <= S_ITEMS or (pair == 1 and q in VECTOR_COPIES):
                nc.vector.tensor_copy(out=dst, in_=src)
            else:
                nc.scalar.copy(out=dst, in_=src)

        def quantise(q):
            if q < S_ITEMS:
                codes[q] = s_codes[:, q, :]
                scales[q] = s_scales[:, q, :]
            else:
                ro_codes = deep.tile([P, HEADS * P], U32, name="ro_codes", align_bytes=64)
                ro_scales = deep.tile([P, HEADS * P], U8, name="ro_scales", align_bytes=64)
                codes[q] = ro_codes[:]
                scales[q] = ro_scales[:]
            nc.vector.quantize_mx(
                out=codes[q].bitcast(FP8X4), scales=scales[q], in_=grouped[q][:]
            )

        def product(q, out_ap, n, h):
            s_item = n * HALVES + q % HALVES
            cols = slice(h * P, (h + 1) * P)
            nc.tensor.matmul_mx(
                out=out_ap,
                lhsT=s_codes[:, s_item, cols].bitcast(FP8X4),
                lhsT_scale=s_scales[:, s_item, cols],
                rhs=codes[q][:, cols].bitcast(FP8X4),
                rhs_scale=scales[q][:, cols],
                start=True,
                stop=True,
            )

        def made_order(q):
            return (0, 1, 2, 3) if (q // HALVES) % 2 == 0 else (1, 0, 3, 2)

        def read_order(q):
            return made_order(q) if q % HALVES == 0 else made_order(q + HALVES)

        def products(q, k):
            b = made_order(q)[k]
            bank = psum_mx.tile([P, 4, P], F32, name=f"dist_{b}")
            dist[q, b] = bank
            for i in range(4):
                if q % HALVES == 0:
                    product(q, bank[:, i, :], b, i)
                else:
                    product(q, bank[:, i, :], i, b)

        def reduce_bank(q, k):
            b = read_order(q)[k]
            m = q // HALVES - S_TILES
            if k == 0:
                best[m] = best_pool.tile([P, S_TILES, P], F32, name="best")
            nc.vector.tensor_reduce(
                out=best[m][:, b, :], in_=dist[q, b][:].rearrange("p h r -> p r h"),
                op=ALU.max, axis=AX.X,
            )

        def link_bank(q, k, parts):
            b = read_order(q)[k]
            m = q // HALVES - S_TILES
            for part in parts:
                nc.vector.tensor_tensor(
                    out=best[m][:, part, :], in0=dist[q, b][:, part, :],
                    in1=best[m][:, part, :], op=ALU.max,
                )
                if k == BANKS - 1:
                    nc.sync.dma_start(
                        out=out_view[:, part, m * P : (m + 1) * P], in_=best[m][:, part, :]
                    )

        whole = (slice(0, S_TILES),)
        halves = (slice(0, S_TILES // 2), slice(S_TILES // 2, S_TILES))

        for t in range(AHEAD):
            load(t)
        pinned.enter_context(tc.manual_schedule())
        for slot in range(ITEMS + 5):
            new = slot
            scaled = slot - 1
            flipping = slot - 2
            turned = slot - 2 if slot - 2 < S_ITEMS else slot - 3
            reduced = slot - 4
            is_new = new < ITEMS
            is_scaled = scaled < ITEMS and slot >= 1
            is_short = is_scaled and scaled < S_ITEMS
            is_long = is_scaled and scaled >= S_ITEMS
            is_flipped = S_ITEMS <= flipping < ITEMS
            is_turned = 0 <= turned < ITEMS and slot != S_ITEMS + 2
            is_multiplied = is_turned and turned >= S_ITEMS
            is_reduced = S_ITEMS <= reduced < ITEMS
            half = reduced % HALVES
            if new % HALVES == 0 and new // HALVES + AHEAD < S_TILES + RO_TILES:
                load(new // HALVES + AHEAD)
            if is_new:
                open_item(new)
                square_on_scalar(new, 0)
            if is_flipped:
                flip(flipping, 0)
                flip(flipping, 1)
            if is_scaled:
                invert_root(scaled)
                open_first_pair(scaled)
            if is_new:
                for h in range(scalar_heads(new), HEADS):
                    square_on_vector(new, h)
            if is_reduced and half == 0:
                reduce_bank(reduced, 0)
            if half == 0 and S_ITEMS < reduced <= ITEMS:
                link_bank(reduced - 1, 3, halves if reduced == ITEMS else whole)
            if is_reduced and half == 0:
                products(reduced, 3)
            if is_turned:
                regroup(turned, 0)
            if is_short:
                scale_pair(scaled, 0)
                flip(scaled, 0)
            if is_turned:
                regroup(turned, 1)
            if is_short:
                open_second_pair(scaled)
                scale_pair(scaled, 1)
                flip(scaled, 1)
            if is_long:
                scale_pair(scaled, 0)
            if is_reduced and half == 1:
                link_bank(reduced, 0, halves if reduced == ITEMS - 1 else whole)
            if is_turned:
                quantise(turned)
            if is_long:
                open_second_pair(scaled)
                scale_pair(scaled, 1)
            if is_new:
                for h in range(1, scalar_heads(new)):
                    square_on_scalar(new, h)
            for k in range(3):
                if is_multiplied:
                    products(turned, k)
                if is_reduced and k < 2:
                    if half == 0:
                        reduce_bank(reduced, k + 1)
                    else:
                        link_bank(reduced, k + 1, halves)
            if is_reduced and half == 0:
                reduce_bank(reduced, 3)
            if is_multiplied and turned % HALVES == 1:
                products(turned, 3)
